import numpy as np
import ml_dtypes


def mxq(x, axis, fmt="e4m3"):
    dtype, down = {"e4m3": (ml_dtypes.float8_e4m3fn, 7), "e5m2": (ml_dtypes.float8_e5m2, 14)}[fmt]
    v = np.moveaxis(np.asarray(x, np.float32).astype(ml_dtypes.bfloat16).astype(np.float64), axis, -1)
    blocks = v.reshape(v.shape[:-1] + (-1, 32))
    amax = np.abs(blocks).max(-1, keepdims=True)
    byte = np.maximum(np.where(amax > 0, np.frexp(amax)[1] - 1 + 127, 0) - down, 1)
    scale = np.exp2(byte - 127.0)
    codes = (blocks / scale).astype(np.float32).astype(dtype).astype(np.float64)
    return np.moveaxis((codes * scale).reshape(v.shape), -1, axis)


WIDE = False


def mx_kscale(k):
    if not WIDE:
        return np.ones(k)
    levels = np.array([10, -10, 5, -5, 0])
    a = np.random.permutation(np.resize(levels, k // 512 * 4)).reshape(k // 512, 4)
    idx = np.arange(k)
    return np.exp2(a[idx // 512, idx % 128 // 32])


BF16 = ml_dtypes.bfloat16


def bf(x):
    return np.asarray(x, np.float32).astype(BF16)


def f64(x):
    return np.asarray(x).astype(np.float64)


B, D0, D1, D2, D3 = 512, 2048, 2048, 2048, 2048
HEBB = 0.01
RATE = 0.001
BATCH_NUM = 1
C = HEBB * RATE / BATCH_NUM


def centred(s):
    return s / np.exp2(np.round(np.log2(s.mean())))


def setup_inputs():
    s = centred(mx_kscale(D2))
    return {"vi": bf(np.maximum(3.0 + 5.0 * np.random.standard_normal((B, D2)), 0.0) * s),
            "W": bf(np.random.standard_normal((D3, D2)) * 0.9 / np.sqrt(D2) / s[None, :]),
            "b": bf(3.0 + 1.5 * np.random.standard_normal(D3))}


def reference(vi, W, b):
    vi = f64(vi)
    vj = np.maximum((mxq(vi, 1, "e4m3") @ mxq(f64(W), 1, "e4m3").T) + f64(b), 0.0)
    m = np.mean(vj, axis=0)
    out = vj + np.sum(vi, axis=1, keepdims=True) * (C * m)[None, :]
    return out, m

@@ -1,0 +1,254 @@
+from contextlib import ExitStack
+
+import concourse.mybir as mybir
+from concourse.masks import make_identity
+
+F32 = mybir.dt.float32
+BF16 = mybir.dt.bfloat16
+U32 = mybir.dt.uint32
+U8 = mybir.dt.uint8
+FP8X4 = mybir.dt.float8_e4m3fn_x4
+ALU = mybir.AluOpType
+ACT = mybir.ActivationFunctionType
+AXIS = mybir.AxisListType
+
+P = 128
+PACK = 4
+K_PASS = P * PACK
+ROWS = 512
+K = 2048
+OUTS = 2048
+PASSES = K // K_PASS
+ROW_TILES = ROWS // P
+OUT_TILES = OUTS // P
+HALVES = 2
+PASSES_PER_BANK = PASSES // HALVES
+WORDS_PER_PASS = K_PASS // 2
+TILE_COLS = PASSES * P * PACK
+
+STEP = 2
+STEPS = OUT_TILES // STEP
+BACK_LAG = 2
+
+C = 0.01 * 0.001 / 1
+FLOPS = 2 * ROWS * K * OUTS
+
+
+def transpose_words(nc, bank, words, half, ident):
+    for i in range(PASSES_PER_BANK):
+        for u in range(2):
+            first = (half * PASSES_PER_BANK + i) * WORDS_PER_PASS + u * P
+            nc.tensor.transpose(bank[:, i, u, :], words[:, first : first + P], ident[:])
+
+
+def tile_optimalnet_pb_kernel(tc, vi, W, b, out_0, out_1):
+    nc = tc.nc
+    with ExitStack() as stack:
+        stack.enter_context(tc.manual_schedule())
+        keep = stack.enter_context(tc.tile_pool(name="keep", bufs=1))
+        weights = stack.enter_context(tc.tile_pool(name="weights", bufs=STEPS))
+        work = stack.enter_context(tc.tile_pool(name="work", bufs=2 * STEP))
+        psum = stack.enter_context(tc.psum_pool(name="psum", bufs=2))
+
+        b_rows = keep.tile([OUT_TILES, P], BF16)
+        nc.scalar.dma_start(out=b_rows[:], in_=b.rearrange("(j p) -> j p", p=P))
+        vi_rows = []
+        for rt in range(ROW_TILES):
+            rows = keep.tile([P, K], BF16, name="vi_rows%d" % rt)
+            nc.sync.dma_start(out=rows[:], in_=vi[rt * P : (rt + 1) * P, :])
+            vi_rows.append(rows)
+        w_rows = []
+        for s in range(STEPS):
+            rows = weights.tile([P, STEP, K], BF16, name="w_rows")
+            first = s * STEP * P
+            nc.sync.dma_start(
+                out=rows[:], in_=W[first : first + STEP * P, :].rearrange("(a p) k -> p a k", p=P)
+            )
+            w_rows.append(rows)
+
+        ident = keep.tile([P, P], F32)
+        make_identity(nc, ident[:])
+        ones = keep.tile([P, P], BF16)
+        nc.vector.memset(ones[:], 1.0)
+        b_square = keep.tile([P, P], F32)
+        nc.vector.memset(b_square[:], 0.0)
+        colsum = keep.tile([P, P], F32)
+        nc.vector.memset(colsum[:], 0.0)
+        nc.vector.tensor_copy(out=b_square[0:OUT_TILES, :], in_=b_rows[:])
+        b_col = keep.tile([P, OUT_TILES], F32)
+
+        vi_grouped = keep.tile([P, PASSES * ROWS * PACK], BF16, align_bytes=64)
+        vi_grouped_words = vi_grouped[:].bitcast(F32).rearrange("p (g r u) -> p g r u", g=PASSES, u=2)
+        vi_grouped_cols = vi_grouped[:].rearrange("p (g c) -> p g c", g=PASSES)
+        vi_codes = keep.tile([P, PASSES, ROWS], U32, align_bytes=64)
+        vi_scales = keep.tile([P, PASSES, ROWS], U8, align_bytes=64)
+        rowsum_raw = keep.tile([P, ROWS], F32)
+        rowsum_scaled = keep.tile([P, ROWS], F32)
+
+        def vi_transpose_and_regroup(rt):
+            for half in range(HALVES):
+                bank = psum.tile([P, PASSES_PER_BANK, 2, P], F32, tag="words", bufs=2 * STEP)
+                transpose_words(nc, bank, vi_rows[rt][:].bitcast(F32), half, ident)
+                nc.scalar.copy(
+                    out=vi_grouped_words[
+                        :, half * PASSES_PER_BANK : (half + 1) * PASSES_PER_BANK, rt * P : (rt + 1) * P, :
+                    ],
+                    in_=bank[:].rearrange("p i u r -> p i r u"),
+                )
+
+        def vi_quantise(rt):
+            for g in range(PASSES):
+                nc.vector.quantize_mx(
+                    out=vi_codes[:, g, rt * P : (rt + 1) * P].bitcast(FP8X4),
+                    scales=vi_scales[:, g, rt * P : (rt + 1) * P],
+                    in_=vi_grouped_cols[:, g, rt * P * PACK : (rt + 1) * P * PACK],
+                )
+
+        def vi_sum_rows(rt):
+            partial = psum.tile([P, P * PACK], F32, tag="product")
+            for g in range(PASSES):
+                nc.tensor.matmul(
+                    out=partial[:],
+                    lhsT=ones[:],
+                    rhs=vi_grouped_cols[:, g, rt * P * PACK : (rt + 1) * P * PACK],
+                    start=(g == 0),
+                    stop=(g == PASSES - 1),
+                )
+            nc.vector.tensor_reduce(
+                out=rowsum_raw[:, rt * P : (rt + 1) * P],
+                in_=partial[:].rearrange("p (r t) -> p r t", t=PACK),
+                axis=AXIS.X,
+                op=ALU.add,
+            )
+
+        w_banks = {}
+        w_grouped = {}
+        w_codes = {}
+        w_scales = {}
+        product = {}
+        vj = {}
+        back = {}
+
+        def tiles_of(s):
+            return range(s * STEP, (s + 1) * STEP)
+
+        def w_transpose(s):
+            for j in tiles_of(s):
+                words = w_rows[s][:, j - s * STEP, :].bitcast(F32)
+                for half in range(HALVES):
+                    bank = psum.tile([P, PASSES_PER_BANK, 2, P], F32, tag="words", bufs=2 * STEP)
+                    transpose_words(nc, bank, words, half, ident)
+                    w_banks[j, half] = bank
+
+        def w_regroup(s):
+            for j in tiles_of(s):
+                w_grouped[j] = work.tile([P, TILE_COLS], BF16, name="w_grouped", align_bytes=64)
+                grouped_words = w_grouped[j][:].bitcast(F32).rearrange("p (g o u) -> p g o u", g=PASSES, u=2)
+                nc.vector.tensor_copy(
+                    out=grouped_words[:, 0:PASSES_PER_BANK],
+                    in_=w_banks[j, 0][:].rearrange("p i u o -> p i o u"),
+                )
+                nc.scalar.copy(
+                    out=grouped_words[:, PASSES_PER_BANK:PASSES],
+                    in_=w_banks[j, 1][:].rearrange("p i u o -> p i o u"),
+                )
+
+        def w_quantise(s):
+            for j in tiles_of(s):
+                w_codes[j] = work.tile([P, PASSES * P], U32, name="w_codes", align_bytes=64)
+                w_scales[j] = work.tile([P, PASSES * P], U8, name="w_scales", align_bytes=64)
+                nc.vector.quantize_mx(
+                    out=w_codes[j][:].bitcast(FP8X4), scales=w_scales[j][:], in_=w_grouped[j][:]
+                )
+
+        def multiply(s):
+            for j in tiles_of(s):
+                product[j] = psum.tile([P, ROWS], F32, name="product", tag="product")
+                for g in range(PASSES):
+                    nc.tensor.matmul_mx(
+                        out=product[j][:],
+                        lhsT=w_codes[j][:, g * P : (g + 1) * P].bitcast(FP8X4),
+                        lhsT_scale=w_scales[j][:, g * P : (g + 1) * P],
+                        rhs=vi_codes[:, g, :].bitcast(FP8X4),
+                        rhs_scale=vi_scales[:, g, :],
+                        start=(g == 0),
+                        stop=(g == PASSES - 1),
+                    )
+
+        def bias_relu_and_sum(s):
+            for j in tiles_of(s):
+                vj[j] = work.tile([P, ROWS], F32, name="vj", bufs=(BACK_LAG + 1) * STEP)
+                nc.scalar.activation(
+                    out=vj[j][:],
+                    in_=product[j][:],
+                    func=ACT.Relu,
+                    bias=b_col[:, j : j + 1],
+                    scale=1.0,
+                    accum_out=colsum[:, j : j + 1],
+                )
+
+        def correct(s):
+            for j in tiles_of(s):
+                nc.vector.scalar_tensor_tensor(
+                    out=vj[j][:],
+                    in0=rowsum_scaled[:],
+                    scalar=colsum[:, j : j + 1],
+                    in1=vj[j][:],
+                    op0=ALU.mult,
+                    op1=ALU.add,
+                )
+
+        def transpose_back(s):
+            for j in tiles_of(s):
+                back[j] = psum.tile([P, ROW_TILES, P], F32, name="back", tag="back")
+                for rt in range(ROW_TILES):
+                    nc.tensor.transpose(back[j][:, rt, :], vj[j][:, rt * P : (rt + 1) * P], ident[:])
+
+        def copy_out_and_store(s):
+            result = work.tile([P, ROW_TILES, STEP * P], F32, name="result", bufs=3)
+            for j in tiles_of(s):
+                first = (j - s * STEP) * P
+                nc.scalar.copy(out=result[:, :, first : first + P], in_=back[j][:])
+            first = s * STEP * P
+            nc.sync.dma_start(
+                out=out_0[:, first : first + STEP * P].rearrange("(t p) o -> p t o", p=P), in_=result[:]
+            )
+
+        def store_mean():
+            sums_as_rows = psum.tile([P, P], F32, tag="back")
+            nc.tensor.transpose(sums_as_rows[:], colsum[:], ident[:])
+            mean_rows = keep.tile([OUT_TILES, P], F32)
+            nc.scalar.mul(out=mean_rows[:], in_=sums_as_rows[0:OUT_TILES, :], mul=1.0 / ROWS)
+            nc.sync.dma_start(out=out_1.rearrange("(j p) -> j p", p=P), in_=mean_rows[:])
+
+        for rt in range(ROW_TILES):
+            vi_transpose_and_regroup(rt)
+            if rt == 0:
+                b_as_columns = psum.tile([P, P], F32, tag="back")
+                nc.tensor.transpose(b_as_columns[:], b_square[:], ident[:])
+                nc.vector.tensor_copy(out=b_col[:], in_=b_as_columns[:, 0:OUT_TILES])
+            else:
+                vi_sum_rows(rt - 1)
+            vi_quantise(rt)
+        w_transpose(0)
+        w_regroup(0)
+        vi_sum_rows(ROW_TILES - 1)
+        nc.vector.tensor_scalar_mul(out=rowsum_scaled[:], in0=rowsum_raw[:], scalar1=C / ROWS)
+        w_quantise(0)
+
+        for i in range(STEPS + BACK_LAG):
+            if i + 1 < STEPS:
+                w_transpose(i + 1)
+                w_regroup(i + 1)
+            if i >= BACK_LAG:
+                transpose_back(i - BACK_LAG)
+                copy_out_and_store(i - BACK_LAG)
+            if i == STEPS:
+                store_mean()
+            if 1 <= i <= STEPS:
+                correct(i - 1)
+            if i + 1 < STEPS:
+                w_quantise(i + 1)
+            if i < STEPS:
+                multiply(i)
+                bias_relu_and_sum(i)

@@ -23,22 +23,32 @@ ROW_TILES = ROWS // P
 OUT_TILES = OUTS // P
 HALVES = 2
 PASSES_PER_BANK = PASSES // HALVES
+K_HALF = K // HALVES
 WORDS_PER_PASS = K_PASS // 2
 TILE_COLS = PASSES * P * PACK
 
 STEP = 2
 STEPS = OUT_TILES // STEP
 BACK_LAG = 2
+PRODUCT_BANKS = STEP
+TRANSPOSE_BANKS = 8 - PRODUCT_BANKS
 
 C = 0.01 * 0.001 / 1
 FLOPS = 2 * ROWS * K * OUTS
 
 
-def transpose_words(nc, bank, words, half, ident):
+def transpose_words(nc, bank, words, ident):
     for i in range(PASSES_PER_BANK):
         for u in range(2):
-            first = (half * PASSES_PER_BANK + i) * WORDS_PER_PASS + u * P
+            first = i * WORDS_PER_PASS + u * P
             nc.tensor.transpose(bank[:, i, u, :], words[:, first : first + P], ident[:])
+
+
+def empty_bank(nc, by_vector, out, in_):
+    if by_vector:
+        nc.vector.tensor_copy(out=out, in_=in_)
+    else:
+        nc.scalar.copy(out=out, in_=in_)
 
 
 def tile_optimalnet_pb_kernel(tc, vi, W, b, out_0, out_1):
@@ -48,15 +58,18 @@ def tile_optimalnet_pb_kernel(tc, vi, W, b, out_0, out_1):
         keep = stack.enter_context(tc.tile_pool(name="keep", bufs=1))
         weights = stack.enter_context(tc.tile_pool(name="weights", bufs=STEPS))
         work = stack.enter_context(tc.tile_pool(name="work", bufs=2 * STEP))
-        psum = stack.enter_context(tc.psum_pool(name="psum", bufs=2))
+        psum = stack.enter_context(tc.psum_pool(name="psum", bufs=PRODUCT_BANKS))
 
         b_rows = keep.tile([OUT_TILES, P], BF16)
         nc.scalar.dma_start(out=b_rows[:], in_=b.rearrange("(j p) -> j p", p=P))
-        vi_rows = []
+        vi_rows = {}
         for rt in range(ROW_TILES):
-            rows = keep.tile([P, K], BF16, name="vi_rows%d" % rt)
-            nc.sync.dma_start(out=rows[:], in_=vi[rt * P : (rt + 1) * P, :])
-            vi_rows.append(rows)
+            for half in range(HALVES):
+                rows = keep.tile([P, K_HALF], BF16, name="vi_rows%d_%d" % (rt, half))
+                nc.sync.dma_start(
+                    out=rows[:], in_=vi[rt * P : (rt + 1) * P, half * K_HALF : (half + 1) * K_HALF]
+                )
+                vi_rows[rt, half] = rows
         w_rows = []
         for s in range(STEPS):
             rows = weights.tile([P, STEP, K], BF16, name="w_rows")
@@ -87,8 +100,8 @@ def tile_optimalnet_pb_kernel(tc, vi, W, b, out_0, out_1):
 
         def vi_transpose_and_regroup(rt):
             for half in range(HALVES):
-                bank = psum.tile([P, PASSES_PER_BANK, 2, P], F32, tag="words", bufs=2 * STEP)
-                transpose_words(nc, bank, vi_rows[rt][:].bitcast(F32), half, ident)
+                bank = psum.tile([P, PASSES_PER_BANK, 2, P], F32, tag="transposed", bufs=TRANSPOSE_BANKS)
+                transpose_words(nc, bank, vi_rows[rt, half][:].bitcast(F32), ident)
                 nc.scalar.copy(
                     out=vi_grouped_words[
                         :, half * PASSES_PER_BANK : (half + 1) * PASSES_PER_BANK, rt * P : (rt + 1) * P, :
@@ -134,24 +147,23 @@ def tile_optimalnet_pb_kernel(tc, vi, W, b, out_0, out_1):
 
         def w_transpose(s):
             for j in tiles_of(s):
-                words = w_rows[s][:, j - s * STEP, :].bitcast(F32)
                 for half in range(HALVES):
-                    bank = psum.tile([P, PASSES_PER_BANK, 2, P], F32, tag="words", bufs=2 * STEP)
-                    transpose_words(nc, bank, words, half, ident)
+                    bank = psum.tile([P, PASSES_PER_BANK, 2, P], F32, tag="transposed", bufs=TRANSPOSE_BANKS)
+                    half_rows = w_rows[s][:, j - s * STEP, half * K_HALF : (half + 1) * K_HALF]
+                    transpose_words(nc, bank, half_rows.bitcast(F32), ident)
                     w_banks[j, half] = bank
 
         def w_regroup(s):
             for j in tiles_of(s):
                 w_grouped[j] = work.tile([P, TILE_COLS], BF16, name="w_grouped", align_bytes=64)
                 grouped_words = w_grouped[j][:].bitcast(F32).rearrange("p (g o u) -> p g o u", g=PASSES, u=2)
-                nc.vector.tensor_copy(
-                    out=grouped_words[:, 0:PASSES_PER_BANK],
-                    in_=w_banks[j, 0][:].rearrange("p i u o -> p i o u"),
-                )
-                nc.scalar.copy(
-                    out=grouped_words[:, PASSES_PER_BANK:PASSES],
-                    in_=w_banks[j, 1][:].rearrange("p i u o -> p i o u"),
-                )
+                for half in range(HALVES):
+                    empty_bank(
+                        nc,
+                        by_vector=(j == s * STEP and half == 0),
+                        out=grouped_words[:, half * PASSES_PER_BANK : (half + 1) * PASSES_PER_BANK],
+                        in_=w_banks[j, half][:].rearrange("p i u o -> p i o u"),
+                    )
 
         def w_quantise(s):
             for j in tiles_of(s):
@@ -200,22 +212,20 @@ def tile_optimalnet_pb_kernel(tc, vi, W, b, out_0, out_1):
 
         def transpose_back(s):
             for j in tiles_of(s):
-                back[j] = psum.tile([P, ROW_TILES, P], F32, name="back", tag="back")
+                back[j] = psum.tile([P, ROW_TILES, P], F32, name="back", tag="transposed", bufs=TRANSPOSE_BANKS)
                 for rt in range(ROW_TILES):
                     nc.tensor.transpose(back[j][:, rt, :], vj[j][:, rt * P : (rt + 1) * P], ident[:])
 
         def copy_out_and_store(s):
-            result = work.tile([P, ROW_TILES, STEP * P], F32, name="result", bufs=3)
             for j in tiles_of(s):
-                first = (j - s * STEP) * P
-                nc.scalar.copy(out=result[:, :, first : first + P], in_=back[j][:])
-            first = s * STEP * P
-            nc.sync.dma_start(
-                out=out_0[:, first : first + STEP * P].rearrange("(t p) o -> p t o", p=P), in_=result[:]
-            )
+                result = work.tile([P, ROW_TILES, P], F32, name="result")
+                empty_bank(nc, by_vector=(j == (s + 1) * STEP - 1), out=result[:], in_=back[j][:])
+                nc.sync.dma_start(
+                    out=out_0[:, j * P : (j + 1) * P].rearrange("(t p) o -> p t o", p=P), in_=result[:]
+                )
 
         def store_mean():
-            sums_as_rows = psum.tile([P, P], F32, tag="back")
+            sums_as_rows = psum.tile([P, P], F32, tag="transposed", bufs=TRANSPOSE_BANKS)
             nc.tensor.transpose(sums_as_rows[:], colsum[:], ident[:])
             mean_rows = keep.tile([OUT_TILES, P], F32)
             nc.scalar.mul(out=mean_rows[:], in_=sums_as_rows[0:OUT_TILES, :], mul=1.0 / ROWS)
@@ -224,7 +234,7 @@ def tile_optimalnet_pb_kernel(tc, vi, W, b, out_0, out_1):
         for rt in range(ROW_TILES):
             vi_transpose_and_regroup(rt)
             if rt == 0:
-                b_as_columns = psum.tile([P, P], F32, tag="back")
+                b_as_columns = psum.tile([P, P], F32, tag="transposed", bufs=TRANSPOSE_BANKS)
                 nc.tensor.transpose(b_as_columns[:], b_square[:], ident[:])
                 nc.vector.tensor_copy(out=b_col[:], in_=b_as_columns[:, 0:OUT_TILES])
             else:
@@ -240,13 +250,13 @@ def tile_optimalnet_pb_kernel(tc, vi, W, b, out_0, out_1):
             if i + 1 < STEPS:
                 w_transpose(i + 1)
                 w_regroup(i + 1)
+            if 1 <= i <= STEPS:
+                correct(i - 1)
             if i >= BACK_LAG:
                 transpose_back(i - BACK_LAG)
                 copy_out_and_store(i - BACK_LAG)
             if i == STEPS:
                 store_mean()
-            if 1 <= i <= STEPS:
-                correct(i - 1)
             if i + 1 < STEPS:
                 w_quantise(i + 1)
             if i < STEPS:

@@ -54,7 +54,6 @@ def empty_bank(nc, by_vector, out, in_):
 def tile_optimalnet_pb_kernel(tc, vi, W, b, out_0, out_1):
     nc = tc.nc
     with ExitStack() as stack:
-        stack.enter_context(tc.manual_schedule())
         keep = stack.enter_context(tc.tile_pool(name="keep", bufs=1))
         weights = stack.enter_context(tc.tile_pool(name="weights", bufs=STEPS))
         work = stack.enter_context(tc.tile_pool(name="work", bufs=2 * STEP))

@@ -56,7 +56,7 @@ def tile_optimalnet_pb_kernel(tc, vi, W, b, out_0, out_1):
     with ExitStack() as stack:
         keep = stack.enter_context(tc.tile_pool(name="keep", bufs=1))
         weights = stack.enter_context(tc.tile_pool(name="weights", bufs=STEPS))
-        work = stack.enter_context(tc.tile_pool(name="work", bufs=2 * STEP))
+        work = stack.enter_context(tc.tile_pool(name="work", bufs=3 * STEP))
         psum = stack.enter_context(tc.psum_pool(name="psum", bufs=PRODUCT_BANKS))
 
         b_rows = keep.tile([OUT_TILES, P], BF16)
@@ -188,7 +188,7 @@ def tile_optimalnet_pb_kernel(tc, vi, W, b, out_0, out_1):
 
         def bias_relu_and_sum(s):
             for j in tiles_of(s):
-                vj[j] = work.tile([P, ROWS], F32, name="vj", bufs=(BACK_LAG + 1) * STEP)
+                vj[j] = work.tile([P, ROWS], F32, name="vj", bufs=(BACK_LAG + 2) * STEP)
                 nc.scalar.activation(
                     out=vj[j][:],
                     in_=product[j][:],

@@ -56,7 +56,7 @@ def tile_optimalnet_pb_kernel(tc, vi, W, b, out_0, out_1):
     with ExitStack() as stack:
         keep = stack.enter_context(tc.tile_pool(name="keep", bufs=1))
         weights = stack.enter_context(tc.tile_pool(name="weights", bufs=STEPS))
-        work = stack.enter_context(tc.tile_pool(name="work", bufs=3 * STEP))
+        work = stack.enter_context(tc.tile_pool(name="work", bufs=2 * STEP))
         psum = stack.enter_context(tc.psum_pool(name="psum", bufs=PRODUCT_BANKS))
 
         b_rows = keep.tile([OUT_TILES, P], BF16)
@@ -80,8 +80,6 @@ def tile_optimalnet_pb_kernel(tc, vi, W, b, out_0, out_1):
 
         ident = keep.tile([P, P], F32)
         make_identity(nc, ident[:])
-        ones = keep.tile([P, P], BF16)
-        nc.vector.memset(ones[:], 1.0)
         b_square = keep.tile([P, P], F32)
         nc.vector.memset(b_square[:], 0.0)
         colsum = keep.tile([P, P], F32)
@@ -94,7 +92,6 @@ def tile_optimalnet_pb_kernel(tc, vi, W, b, out_0, out_1):
         vi_grouped_cols = vi_grouped[:].rearrange("p (g c) -> p g c", g=PASSES)
         vi_codes = keep.tile([P, PASSES, ROWS], U32, align_bytes=64)
         vi_scales = keep.tile([P, PASSES, ROWS], U8, align_bytes=64)
-        rowsum_raw = keep.tile([P, ROWS], F32)
         rowsum_scaled = keep.tile([P, ROWS], F32)
 
         def vi_transpose_and_regroup(rt):
@@ -116,22 +113,32 @@ def tile_optimalnet_pb_kernel(tc, vi, W, b, out_0, out_1):
                     in_=vi_grouped_cols[:, g, rt * P * PACK : (rt + 1) * P * PACK],
                 )
 
-        def vi_sum_rows(rt):
-            partial = psum.tile([P, P * PACK], F32, tag="product")
-            for g in range(PASSES):
-                nc.tensor.matmul(
-                    out=partial[:],
-                    lhsT=ones[:],
-                    rhs=vi_grouped_cols[:, g, rt * P * PACK : (rt + 1) * P * PACK],
-                    start=(g == 0),
-                    stop=(g == PASSES - 1),
+        def vi_sum_rows():
+            first_half_sums = keep.tile([P, ROW_TILES], F32)
+            second_half_sums = keep.tile([P, ROW_TILES], F32)
+            unread = keep.tile([P, ROW_TILES, K_HALF], BF16)
+            for rt in range(ROW_TILES):
+                nc.vector.tensor_reduce(
+                    out=first_half_sums[:, rt : rt + 1], in_=vi_rows[rt, 0][:], axis=AXIS.X, op=ALU.add
                 )
-            nc.vector.tensor_reduce(
-                out=rowsum_raw[:, rt * P : (rt + 1) * P],
-                in_=partial[:].rearrange("p (r t) -> p r t", t=PACK),
-                axis=AXIS.X,
-                op=ALU.add,
+                nc.scalar.activation(
+                    out=unread[:, rt, :],
+                    in_=vi_rows[rt, 1][:],
+                    func=ACT.Copy,
+                    accum_out=second_half_sums[:, rt : rt + 1],
+                )
+            rowsum = keep.tile([P, ROW_TILES], F32)
+            nc.vector.tensor_tensor(out=rowsum[:], in0=first_half_sums[:], in1=second_half_sums[:], op=ALU.add)
+            repeated = keep.tile([P, ROW_TILES, P], F32)
+            nc.vector.tensor_scalar_mul(
+                out=repeated[:],
+                in0=rowsum[:].unsqueeze(2).to_broadcast([P, ROW_TILES, P]),
+                scalar1=C / ROWS,
             )
+            spread = psum.tile([P, ROW_TILES, P], F32, tag="transposed", bufs=TRANSPOSE_BANKS)
+            for rt in range(ROW_TILES):
+                nc.tensor.transpose(spread[:, rt, :], repeated[:, rt, :], ident[:])
+            nc.vector.tensor_copy(out=rowsum_scaled[:], in_=spread[:].rearrange("p t r -> p (t r)"))
 
         w_banks = {}
         w_grouped = {}
@@ -188,7 +195,7 @@ def tile_optimalnet_pb_kernel(tc, vi, W, b, out_0, out_1):
 
         def bias_relu_and_sum(s):
             for j in tiles_of(s):
-                vj[j] = work.tile([P, ROWS], F32, name="vj", bufs=(BACK_LAG + 2) * STEP)
+                vj[j] = work.tile([P, ROWS], F32, name="vj", bufs=(BACK_LAG + 1) * STEP)
                 nc.scalar.activation(
                     out=vj[j][:],
                     in_=product[j][:],
@@ -232,18 +239,14 @@ def tile_optimalnet_pb_kernel(tc, vi, W, b, out_0, out_1):
 
         for rt in range(ROW_TILES):
             vi_transpose_and_regroup(rt)
-            if rt == 0:
-                b_as_columns = psum.tile([P, P], F32, tag="transposed", bufs=TRANSPOSE_BANKS)
-                nc.tensor.transpose(b_as_columns[:], b_square[:], ident[:])
-                nc.vector.tensor_copy(out=b_col[:], in_=b_as_columns[:, 0:OUT_TILES])
-            else:
-                vi_sum_rows(rt - 1)
             vi_quantise(rt)
         w_transpose(0)
         w_regroup(0)
-        vi_sum_rows(ROW_TILES - 1)
-        nc.vector.tensor_scalar_mul(out=rowsum_scaled[:], in0=rowsum_raw[:], scalar1=C / ROWS)
         w_quantise(0)
+        b_as_columns = psum.tile([P, P], F32, tag="transposed", bufs=TRANSPOSE_BANKS)
+        nc.tensor.transpose(b_as_columns[:], b_square[:], ident[:])
+        nc.vector.tensor_copy(out=b_col[:], in_=b_as_columns[:, 0:OUT_TILES])
+        vi_sum_rows()
 
         for i in range(STEPS + BACK_LAG):
             if i + 1 < STEPS:

from contextlib import ExitStack

import concourse.mybir as mybir
from concourse.masks import make_identity

F32 = mybir.dt.float32
BF16 = mybir.dt.bfloat16
U32 = mybir.dt.uint32
U8 = mybir.dt.uint8
FP8X4 = mybir.dt.float8_e4m3fn_x4
ALU = mybir.AluOpType
ACT = mybir.ActivationFunctionType
AXIS = mybir.AxisListType

P = 128
PACK = 4
K_PASS = P * PACK
ROWS = 512
K = 2048
OUTS = 2048
PASSES = K // K_PASS
ROW_TILES = ROWS // P
OUT_TILES = OUTS // P
HALVES = 2
PASSES_PER_BANK = PASSES // HALVES
K_HALF = K // HALVES
WORDS_PER_PASS = K_PASS // 2
TILE_COLS = PASSES * P * PACK

STEP = 2
STEPS = OUT_TILES // STEP
BACK_LAG = 2
PRODUCT_BANKS = STEP
TRANSPOSE_BANKS = 8 - PRODUCT_BANKS

C = 0.01 * 0.001 / 1
FLOPS = 2 * ROWS * K * OUTS


def transpose_words(nc, bank, words, ident):
    for i in range(PASSES_PER_BANK):
        for u in range(2):
            first = i * WORDS_PER_PASS + u * P
            nc.tensor.transpose(bank[:, i, u, :], words[:, first : first + P], ident[:])


def empty_bank(nc, by_vector, out, in_):
    if by_vector:
        nc.vector.tensor_copy(out=out, in_=in_)
    else:
        nc.scalar.copy(out=out, in_=in_)


def tile_optimalnet_pb_kernel(tc, vi, W, b, out_0, out_1):
    nc = tc.nc
    with ExitStack() as stack:
        keep = stack.enter_context(tc.tile_pool(name="keep", bufs=1))
        weights = stack.enter_context(tc.tile_pool(name="weights", bufs=STEPS))
        work = stack.enter_context(tc.tile_pool(name="work", bufs=2 * STEP))
        psum = stack.enter_context(tc.psum_pool(name="psum", bufs=PRODUCT_BANKS))

        b_rows = keep.tile([OUT_TILES, P], BF16)
        nc.scalar.dma_start(out=b_rows[:], in_=b.rearrange("(j p) -> j p", p=P))
        vi_rows = {}
        for rt in range(ROW_TILES):
            for half in range(HALVES):
                rows = keep.tile([P, K_HALF], BF16, name="vi_rows%d_%d" % (rt, half))
                nc.sync.dma_start(
                    out=rows[:], in_=vi[rt * P : (rt + 1) * P, half * K_HALF : (half + 1) * K_HALF]
                )
                vi_rows[rt, half] = rows
        w_rows = []
        for s in range(STEPS):
            rows = weights.tile([P, STEP, K], BF16, name="w_rows")
            first = s * STEP * P
            nc.sync.dma_start(
                out=rows[:], in_=W[first : first + STEP * P, :].rearrange("(a p) k -> p a k", p=P)
            )
            w_rows.append(rows)

        ident = keep.tile([P, P], F32)
        make_identity(nc, ident[:])
        b_square = keep.tile([P, P], F32)
        nc.vector.memset(b_square[:], 0.0)
        colsum = keep.tile([P, P], F32)
        nc.vector.memset(colsum[:], 0.0)
        nc.vector.tensor_copy(out=b_square[0:OUT_TILES, :], in_=b_rows[:])
        b_col = keep.tile([P, OUT_TILES], F32)

        vi_grouped = keep.tile([P, PASSES * ROWS * PACK], BF16, align_bytes=64)
        vi_grouped_words = vi_grouped[:].bitcast(F32).rearrange("p (g r u) -> p g r u", g=PASSES, u=2)
        vi_grouped_cols = vi_grouped[:].rearrange("p (g c) -> p g c", g=PASSES)
        vi_codes = keep.tile([P, PASSES, ROWS], U32, align_bytes=64)
        vi_scales = keep.tile([P, PASSES, ROWS], U8, align_bytes=64)
        rowsum_scaled = keep.tile([P, ROWS], F32)

        def vi_transpose_and_regroup(rt):
            for half in range(HALVES):
                bank = psum.tile([P, PASSES_PER_BANK, 2, P], F32, tag="transposed", bufs=TRANSPOSE_BANKS)
                transpose_words(nc, bank, vi_rows[rt, half][:].bitcast(F32), ident)
                nc.scalar.copy(
                    out=vi_grouped_words[
                        :, half * PASSES_PER_BANK : (half + 1) * PASSES_PER_BANK, rt * P : (rt + 1) * P, :
                    ],
                    in_=bank[:].rearrange("p i u r -> p i r u"),
                )

        def vi_quantise(rt):
            for g in range(PASSES):
                nc.vector.quantize_mx(
                    out=vi_codes[:, g, rt * P : (rt + 1) * P].bitcast(FP8X4),
                    scales=vi_scales[:, g, rt * P : (rt + 1) * P],
                    in_=vi_grouped_cols[:, g, rt * P * PACK : (rt + 1) * P * PACK],
                )

        def vi_sum_rows():
            first_half_sums = keep.tile([P, ROW_TILES], F32)
            second_half_sums = keep.tile([P, ROW_TILES], F32)
            unread = keep.tile([P, ROW_TILES, K_HALF], BF16)
            for rt in range(ROW_TILES):
                nc.vector.tensor_reduce(
                    out=first_half_sums[:, rt : rt + 1], in_=vi_rows[rt, 0][:], axis=AXIS.X, op=ALU.add
                )
                nc.scalar.activation(
                    out=unread[:, rt, :],
                    in_=vi_rows[rt, 1][:],
                    func=ACT.Copy,
                    accum_out=second_half_sums[:, rt : rt + 1],
                )
            rowsum = keep.tile([P, ROW_TILES], F32)
            nc.vector.tensor_tensor(out=rowsum[:], in0=first_half_sums[:], in1=second_half_sums[:], op=ALU.add)
            repeated = keep.tile([P, ROW_TILES, P], F32)
            nc.vector.tensor_scalar_mul(
                out=repeated[:],
                in0=rowsum[:].unsqueeze(2).to_broadcast([P, ROW_TILES, P]),
                scalar1=C / ROWS,
            )
            spread = psum.tile([P, ROW_TILES, P], F32, tag="transposed", bufs=TRANSPOSE_BANKS)
            for rt in range(ROW_TILES):
                nc.tensor.transpose(spread[:, rt, :], repeated[:, rt, :], ident[:])
            nc.vector.tensor_copy(out=rowsum_scaled[:], in_=spread[:].rearrange("p t r -> p (t r)"))

        w_banks = {}
        w_grouped = {}
        w_codes = {}
        w_scales = {}
        product = {}
        vj = {}
        back = {}

        def tiles_of(s):
            return range(s * STEP, (s + 1) * STEP)

        def w_transpose(s):
            for j in tiles_of(s):
                for half in range(HALVES):
                    bank = psum.tile([P, PASSES_PER_BANK, 2, P], F32, tag="transposed", bufs=TRANSPOSE_BANKS)
                    half_rows = w_rows[s][:, j - s * STEP, half * K_HALF : (half + 1) * K_HALF]
                    transpose_words(nc, bank, half_rows.bitcast(F32), ident)
                    w_banks[j, half] = bank

        def w_regroup(s):
            for j in tiles_of(s):
                w_grouped[j] = work.tile([P, TILE_COLS], BF16, name="w_grouped", align_bytes=64)
                grouped_words = w_grouped[j][:].bitcast(F32).rearrange("p (g o u) -> p g o u", g=PASSES, u=2)
                for half in range(HALVES):
                    empty_bank(
                        nc,
                        by_vector=(j == s * STEP and half == 0),
                        out=grouped_words[:, half * PASSES_PER_BANK : (half + 1) * PASSES_PER_BANK],
                        in_=w_banks[j, half][:].rearrange("p i u o -> p i o u"),
                    )

        def w_quantise(s):
            for j in tiles_of(s):
                w_codes[j] = work.tile([P, PASSES * P], U32, name="w_codes", align_bytes=64)
                w_scales[j] = work.tile([P, PASSES * P], U8, name="w_scales", align_bytes=64)
                nc.vector.quantize_mx(
                    out=w_codes[j][:].bitcast(FP8X4), scales=w_scales[j][:], in_=w_grouped[j][:]
                )

        def multiply(s):
            for j in tiles_of(s):
                product[j] = psum.tile([P, ROWS], F32, name="product", tag="product")
                for g in range(PASSES):
                    nc.tensor.matmul_mx(
                        out=product[j][:],
                        lhsT=w_codes[j][:, g * P : (g + 1) * P].bitcast(FP8X4),
                        lhsT_scale=w_scales[j][:, g * P : (g + 1) * P],
                        rhs=vi_codes[:, g, :].bitcast(FP8X4),
                        rhs_scale=vi_scales[:, g, :],
                        start=(g == 0),
                        stop=(g == PASSES - 1),
                    )

        def bias_relu_and_sum(s):
            for j in tiles_of(s):
                vj[j] = work.tile([P, ROWS], F32, name="vj", bufs=(BACK_LAG + 1) * STEP)
                nc.scalar.activation(
                    out=vj[j][:],
                    in_=product[j][:],
                    func=ACT.Relu,
                    bias=b_col[:, j : j + 1],
                    scale=1.0,
                    accum_out=colsum[:, j : j + 1],
                )

        def correct(s):
            for j in tiles_of(s):
                nc.vector.scalar_tensor_tensor(
                    out=vj[j][:],
                    in0=rowsum_scaled[:],
                    scalar=colsum[:, j : j + 1],
                    in1=vj[j][:],
                    op0=ALU.mult,
                    op1=ALU.add,
                )

        def transpose_back(s):
            for j in tiles_of(s):
                back[j] = psum.tile([P, ROW_TILES, P], F32, name="back", tag="transposed", bufs=TRANSPOSE_BANKS)
                for rt in range(ROW_TILES):
                    nc.tensor.transpose(back[j][:, rt, :], vj[j][:, rt * P : (rt + 1) * P], ident[:])

        def copy_out_and_store(s):
            for j in tiles_of(s):
                result = work.tile([P, ROW_TILES, P], F32, name="result")
                empty_bank(nc, by_vector=(j == (s + 1) * STEP - 1), out=result[:], in_=back[j][:])
                nc.sync.dma_start(
                    out=out_0[:, j * P : (j + 1) * P].rearrange("(t p) o -> p t o", p=P), in_=result[:]
                )

        def store_mean():
            sums_as_rows = psum.tile([P, P], F32, tag="transposed", bufs=TRANSPOSE_BANKS)
            nc.tensor.transpose(sums_as_rows[:], colsum[:], ident[:])
            mean_rows = keep.tile([OUT_TILES, P], F32)
            nc.scalar.mul(out=mean_rows[:], in_=sums_as_rows[0:OUT_TILES, :], mul=1.0 / ROWS)
            nc.sync.dma_start(out=out_1.rearrange("(j p) -> j p", p=P), in_=mean_rows[:])

        for rt in range(ROW_TILES):
            vi_transpose_and_regroup(rt)
            vi_quantise(rt)
        w_transpose(0)
        w_regroup(0)
        w_quantise(0)
        b_as_columns = psum.tile([P, P], F32, tag="transposed", bufs=TRANSPOSE_BANKS)
        nc.tensor.transpose(b_as_columns[:], b_square[:], ident[:])
        nc.vector.tensor_copy(out=b_col[:], in_=b_as_columns[:, 0:OUT_TILES])
        vi_sum_rows()

        for i in range(STEPS + BACK_LAG):
            if i + 1 < STEPS:
                w_transpose(i + 1)
                w_regroup(i + 1)
            if 1 <= i <= STEPS:
                correct(i - 1)
            if i >= BACK_LAG:
                transpose_back(i - BACK_LAG)
                copy_out_and_store(i - BACK_LAG)
            if i == STEPS:
                store_mean()
            if i + 1 < STEPS:
                w_quantise(i + 1)
            if i < STEPS:
                multiply(i)
                bias_relu_and_sum(i)
